import numpy as np
import ml_dtypes


def mxq(x, axis, fmt="e4m3"):
    dtype, down = {"e4m3": (ml_dtypes.float8_e4m3fn, 7), "e5m2": (ml_dtypes.float8_e5m2, 14)}[fmt]
    v = np.moveaxis(np.asarray(x, np.float32).astype(ml_dtypes.bfloat16).astype(np.float64), axis, -1)
    blocks = v.reshape(v.shape[:-1] + (-1, 32))
    amax = np.abs(blocks).max(-1, keepdims=True)
    byte = np.maximum(np.where(amax > 0, np.frexp(amax)[1] - 1 + 127, 0) - down, 1)
    scale = np.exp2(byte - 127.0)
    codes = (blocks / scale).astype(np.float32).astype(dtype).astype(np.float64)
    return np.moveaxis((codes * scale).reshape(v.shape), -1, axis)


WIDE = False


def mx_kscale(k):
    if not WIDE:
        return np.ones(k)
    levels = np.array([10, -10, 5, -5, 0])
    a = np.random.permutation(np.resize(levels, k // 512 * 4)).reshape(k // 512, 4)
    idx = np.arange(k)
    return np.exp2(a[idx // 512, idx % 128 // 32])


BF16 = ml_dtypes.bfloat16


def bf(x):
    return np.asarray(x, np.float32).astype(BF16)


def f64(x):
    return np.asarray(x).astype(np.float64)


E2M1 = np.array([0.0, 0.5, 1.0, 1.5, 2.0, 3.0, 4.0, 6.0, -0.0, -0.5, -1.0, -1.5, -2.0, -3.0, -4.0, -6.0])


def pack_weight(w, fmt):
    k, n = w.shape
    w = f64(bf(w)).reshape(k // 32, 32, n)
    amax = np.abs(w).max(1)
    if fmt == "e4m3":
        byte = np.frexp(amax)[1] - 1 + 127 - 7
    else:
        mant, ex = np.frexp(amax / 6.0)
        byte = np.where(mant > 0.5, ex, ex - 1) + 127
    byte = np.clip(np.where(amax > 0, byte, 1), 1, 254)
    scaled = (w * np.exp2(127.0 - byte)[:, None, :]).reshape(k, n).astype(np.float32)
    by_word = np.ascontiguousarray(scaled.reshape(k // 512, 128, 4, n).transpose(0, 1, 3, 2))
    if fmt == "e4m3":
        words = by_word.astype(ml_dtypes.float8_e4m3fn).view(np.uint8)
    else:
        c = by_word.astype(ml_dtypes.float4_e2m1fn).view(np.uint8) & 0xF
        words = c[..., 0::2] | (c[..., 1::2] << 4)
    return np.ascontiguousarray(words), np.ascontiguousarray(byte.astype(np.uint8).reshape(k // 512, 16, n))


def unpack_weight(words, scales, fmt):
    g, p, n, _ = words.shape
    if fmt == "e4m3":
        vals = np.ascontiguousarray(words).view(ml_dtypes.float8_e4m3fn).astype(np.float64)
    else:
        nib = np.empty((g, p, n, 4), np.uint8)
        nib[..., 0::2] = words & 0xF
        nib[..., 1::2] = words >> 4
        vals = E2M1[nib]
    vals = vals * np.repeat(np.exp2(scales.astype(np.float64) - 127.0), 8, axis=1)[..., None]
    return vals.transpose(0, 1, 3, 2).reshape(g * 512, n)

def pack4(w):
    words, scales = pack_weight(w, "e2m1")
    return words.reshape(words.shape[0], 128, -1), scales


def unpack4(words, scales):
    return unpack_weight(words.reshape(words.shape[0], 128, -1, 2), scales, "e2m1")


B, T, E, V, H, C = 2, 2048, 512, 2048, 4, 512
KD = E // H
ROPE_BASE = 10000.0


def rotate_every_two(u):
    u1 = u[..., ::2]
    u2 = u[..., 1::2]
    return np.stack((-u2, u1), axis=-1).reshape(u.shape)


def theta_shift(u, sin, cos):
    return u * cos + rotate_every_two(u) * sin


def setup_inputs():
    s = mx_kscale(E)
    angle = np.arange(T)[:, None] * (1.0 / ROPE_BASE ** (np.repeat(np.arange(KD // 2), 2) * 2.0 / KD))
    x = bf(np.random.standard_normal((B, T, E)) * s)
    sin = bf(np.sin(angle))
    cos = bf(np.cos(angle))
    Wq_words, Wq_scales = pack4(np.random.standard_normal((E, E)) * 0.5 / np.sqrt(E) / s[:, None])
    Wk_words, Wk_scales = pack4(np.random.standard_normal((E, E)) * 2.0 / np.sqrt(E) / s[:, None])
    return {"x": x,
            "sin": sin, "cos": cos,
            "Wq_words": Wq_words, "Wq_scales": Wq_scales,
            "Wk_words": Wk_words, "Wk_scales": Wk_scales}


def reference(x, sin, cos, Wq_words, Wq_scales, Wk_words, Wk_scales):
    xq = mxq(f64(x), 2, "e4m3")
    q = (xq @ unpack4(Wq_words, Wq_scales)).reshape(B, T, H, KD).transpose(0, 2, 1, 3)
    k = ((xq @ unpack4(Wk_words, Wk_scales)) * KD ** -0.5).reshape(B, T, H, KD).transpose(0, 2, 1, 3)
    return theta_shift(q, f64(sin), f64(cos)), theta_shift(k, f64(sin), f64(cos))

@@ -1,0 +1,162 @@
+from contextlib import ExitStack
+
+import concourse.mybir as mybir
+from concourse.masks import make_identity
+
+F32 = mybir.dt.float32
+BF16 = mybir.dt.bfloat16
+I32 = mybir.dt.int32
+U32 = mybir.dt.uint32
+U8 = mybir.dt.uint8
+FP8X4 = mybir.dt.float8_e4m3fn_x4
+FP4X4 = mybir.dt.float4_e2m1fn_x4
+MULT = mybir.AluOpType.mult
+ADD = mybir.AluOpType.add
+
+P = 128
+BATCH, SEQ, EMBED, HEADS = 2, 2048, 512, 4
+HEAD_DIM = EMBED // HEADS
+PAIRS = HEAD_DIM // 2
+TILES = SEQ // P
+GROUP = 2
+WORDS = EMBED // 2
+OUT_SCALE = (1.0, HEAD_DIM**-0.5)
+
+FLOPS = 2 * BATCH * SEQ * EMBED * 2 * EMBED
+
+
+def tile_multiscaleretention_pa_t_kernel(
+    tc, x, sin, cos, Wq_words, Wq_scales, Wk_words, Wk_scales, out_0, out_1
+):
+    nc = tc.nc
+    groups = [(first, b) for first in range(0, TILES, GROUP) for b in range(BATCH)]
+
+    with ExitStack() as ctx:
+        keep = ctx.enter_context(tc.tile_pool(name="keep", bufs=1))
+        stage = ctx.enter_context(tc.tile_pool(name="stage", bufs=3))
+        work = ctx.enter_context(tc.tile_pool(name="work", bufs=3))
+        results = ctx.enter_context(tc.tile_pool(name="results", bufs=4))
+        psum_t = ctx.enter_context(tc.psum_pool(name="psum_t", bufs=2))
+        psum_u = ctx.enter_context(tc.psum_pool(name="psum_u", bufs=6))
+
+        x_sb = keep.tile([P, BATCH, TILES, EMBED], BF16)
+        cos_sb = keep.tile([P, TILES, HEAD_DIM], BF16)
+        sin_sb = keep.tile([P, TILES, HEAD_DIM], BF16)
+        factors = keep.tile([P, 2, TILES, HEAD_DIM], BF16)
+        w_words = keep.tile([P, 2, 2 * EMBED], U8, align_bytes=64)
+        w_scales = keep.tile([P, 2, EMBED], U8, align_bytes=64)
+        ident = keep.tile([P, P], F32)
+
+        x_rows = x.rearrange("b (p j) k -> b p j k", j=TILES)
+        cos_rows = cos.rearrange("(p j) c -> p j c", j=TILES)
+        sin_rows = sin.rearrange("(p j) c -> p j c", j=TILES)
+
+        def load_group(n):
+            first, b = groups[n]
+            rows = slice(first, first + GROUP)
+            nc.sync.dma_start(out=x_sb[:, b, rows, :], in_=x_rows[b, :, rows, :])
+            if b == 0:
+                nc.sync.dma_start(out=cos_sb[:, rows, :], in_=cos_rows[:, rows, :])
+                nc.sync.dma_start(out=sin_sb[:, rows, :], in_=sin_rows[:, rows, :])
+
+        def load_weight(w, words, scales):
+            nc.sync.dma_start(out=w_words[:, w, :].bitcast(I32), in_=words[0].bitcast(I32))
+            for quad in range(4):
+                nc.sync.dma_start(
+                    out=w_scales[32 * quad : 32 * quad + 4, w, :].bitcast(I32),
+                    in_=scales[0, 4 * quad : 4 * quad + 4, :].bitcast(I32),
+                )
+
+        nc.vector.memset(w_scales[:].bitcast(I32), 0)
+        make_identity(nc, ident[:])
+
+        load_group(0)
+        load_weight(0, Wq_words, Wq_scales)
+        load_weight(1, Wk_words, Wk_scales)
+        for n in range(1, len(groups)):
+            load_group(n)
+
+        grouped_of = {}
+        codes_of = {}
+
+        def build_factors(rows):
+            even = slice(0, HEAD_DIM, 2)
+            odd = slice(1, HEAD_DIM, 2)
+            nc.scalar.copy(out=factors[:, 0, rows, even], in_=cos_sb[:, rows, even])
+            nc.scalar.copy(out=factors[:, 0, rows, odd], in_=sin_sb[:, rows, odd])
+            nc.scalar.mul(out=factors[:, 1, rows, even], in_=sin_sb[:, rows, even], mul=-1.0)
+            nc.scalar.copy(out=factors[:, 1, rows, odd], in_=cos_sb[:, rows, odd])
+
+        def regroup(n):
+            first, b = groups[n]
+            xt = psum_t.tile([P, GROUP, 2, P], F32)
+            for j in range(GROUP):
+                words = x_sb[:, b, first + j, :].bitcast(F32)
+                for half in range(2):
+                    nc.tensor.transpose(xt[:, j, half, :], words[:, half:WORDS:2], ident[:])
+            grouped = stage.tile([P, GROUP * P * 4], BF16, align_bytes=64)
+            nc.scalar.copy(
+                out=grouped[:].bitcast(F32).rearrange("p (j t h) -> p j t h", j=GROUP, h=2),
+                in_=xt[:].rearrange("p j h t -> p j t h"),
+            )
+            grouped_of[n] = grouped
+            if b == 0:
+                build_factors(slice(first, first + GROUP))
+
+        def quantise(n):
+            codes = stage.tile([P, GROUP * P], U32, align_bytes=64)
+            scales = stage.tile([P, GROUP * P], U8, align_bytes=64)
+            nc.vector.quantize_mx(
+                out=codes[:].bitcast(FP8X4), scales=scales[:], in_=grouped_of[n][:]
+            )
+            codes_of[n] = (codes, scales)
+
+        def project_and_rotate(n):
+            first, b = groups[n]
+            codes, scales = codes_of[n]
+            rows = slice(first, first + GROUP)
+            for w, dst in enumerate((out_0, out_1)):
+                products = work.tile([P, 2, HEADS, GROUP, HEAD_DIM], F32)
+                for j in range(GROUP):
+                    tokens = slice(j * P, (j + 1) * P)
+                    u = psum_u.tile([P, EMBED], F32)
+                    nc.tensor.matmul_mx(
+                        out=u[:],
+                        lhsT=codes[:, tokens].bitcast(FP8X4),
+                        lhsT_scale=scales[:, tokens],
+                        rhs=w_words[:, w, :].bitcast(FP4X4),
+                        rhs_scale=w_scales[:, w, :],
+                        start=True,
+                        stop=True,
+                    )
+                    pairs = u[:].rearrange("p (h i e) -> p h i e", h=HEADS, e=2)
+                    for e in range(2):
+                        nc.vector.scalar_tensor_tensor(
+                            out=products[:, e, :, j, :].rearrange("p h (i r) -> p h i r", r=2),
+                            in0=pairs[:, :, :, e : e + 1].to_broadcast([P, HEADS, PAIRS, 2]),
+                            scalar=OUT_SCALE[w],
+                            in1=factors[:, e, first + j, :]
+                            .rearrange("p (i r) -> p i r", r=2)
+                            .unsqueeze(1)
+                            .to_broadcast([P, HEADS, PAIRS, 2]),
+                            op0=MULT,
+                            op1=MULT,
+                        )
+                rotated = results.tile([P, HEADS, GROUP, HEAD_DIM], F32)
+                nc.gpsimd.tensor_tensor(
+                    out=rotated[:], in0=products[:, 0], in1=products[:, 1], op=ADD
+                )
+                nc.sync.dma_start(
+                    out=dst[b].rearrange("h (p j) c -> p h j c", j=TILES)[:, :, rows, :],
+                    in_=rotated[:],
+                )
+
+        regroup(0)
+        regroup(1)
+        quantise(0)
+        for n in range(len(groups)):
+            if n + 2 < len(groups):
+                regroup(n + 2)
+            if n + 1 < len(groups):
+                quantise(n + 1)
+            project_and_rotate(n)

@@ -42,7 +42,7 @@ def tile_multiscaleretention_pa_t_kernel(
         x_sb = keep.tile([P, BATCH, TILES, EMBED], BF16)
         cos_sb = keep.tile([P, TILES, HEAD_DIM], BF16)
         sin_sb = keep.tile([P, TILES, HEAD_DIM], BF16)
-        factors = keep.tile([P, 2, TILES, HEAD_DIM], BF16)
+        factors = keep.tile([P, 2, 2, TILES, HEAD_DIM], F32)
         w_words = keep.tile([P, 2, 2 * EMBED], U8, align_bytes=64)
         w_scales = keep.tile([P, 2, EMBED], U8, align_bytes=64)
         ident = keep.tile([P, P], F32)
@@ -82,10 +82,11 @@ def tile_multiscaleretention_pa_t_kernel(
         def build_factors(rows):
             even = slice(0, HEAD_DIM, 2)
             odd = slice(1, HEAD_DIM, 2)
-            nc.scalar.copy(out=factors[:, 0, rows, even], in_=cos_sb[:, rows, even])
-            nc.scalar.copy(out=factors[:, 0, rows, odd], in_=sin_sb[:, rows, odd])
-            nc.scalar.mul(out=factors[:, 1, rows, even], in_=sin_sb[:, rows, even], mul=-1.0)
-            nc.scalar.copy(out=factors[:, 1, rows, odd], in_=cos_sb[:, rows, odd])
+            for w, scale in enumerate(OUT_SCALE):
+                nc.scalar.mul(out=factors[:, w, 0, rows, even], in_=cos_sb[:, rows, even], mul=scale)
+                nc.scalar.mul(out=factors[:, w, 0, rows, odd], in_=sin_sb[:, rows, odd], mul=scale)
+                nc.scalar.mul(out=factors[:, w, 1, rows, even], in_=sin_sb[:, rows, even], mul=-scale)
+                nc.scalar.mul(out=factors[:, w, 1, rows, odd], in_=cos_sb[:, rows, odd], mul=scale)
 
         def regroup(n):
             first, b = groups[n]
@@ -129,19 +130,19 @@ def tile_multiscaleretention_pa_t_kernel(
                         start=True,
                         stop=True,
                     )
-                    pairs = u[:].rearrange("p (h i e) -> p h i e", h=HEADS, e=2)
-                    for e in range(2):
-                        nc.vector.scalar_tensor_tensor(
-                            out=products[:, e, :, j, :].rearrange("p h (i r) -> p h i r", r=2),
-                            in0=pairs[:, :, :, e : e + 1].to_broadcast([P, HEADS, PAIRS, 2]),
-                            scalar=OUT_SCALE[w],
-                            in1=factors[:, e, first + j, :]
-                            .rearrange("p (i r) -> p i r", r=2)
-                            .unsqueeze(1)
-                            .to_broadcast([P, HEADS, PAIRS, 2]),
-                            op0=MULT,
-                            op1=MULT,
-                        )
+                    shape = [P, 2, HEADS, PAIRS, 2]
+                    nc.vector.tensor_tensor(
+                        out=products[:, :, :, j, :].rearrange("p e h (i r) -> p e h i r", r=2),
+                        in0=u[:]
+                        .rearrange("p (h i e) -> p e h i", h=HEADS, e=2)
+                        .unsqueeze(4)
+                        .to_broadcast(shape),
+                        in1=factors[:, w, :, first + j, :]
+                        .rearrange("p e (i r) -> p e i r", r=2)
+                        .unsqueeze(2)
+                        .to_broadcast(shape),
+                        op=MULT,
+                    )
                 rotated = results.tile([P, HEADS, GROUP, HEAD_DIM], F32)
                 nc.gpsimd.tensor_tensor(
                     out=rotated[:], in0=products[:, 0], in1=products[:, 1], op=ADD

@@ -18,7 +18,9 @@ BATCH, SEQ, EMBED, HEADS = 2, 2048, 512, 4
 HEAD_DIM = EMBED // HEADS
 PAIRS = HEAD_DIM // 2
 TILES = SEQ // P
-GROUP = 2
+GROUP = 4
+BANK_TILES = 2
+VECTOR_ADDS = 1
 WORDS = EMBED // 2
 OUT_SCALE = (1.0, HEAD_DIM**-0.5)
 
@@ -42,7 +44,7 @@ def tile_multiscaleretention_pa_t_kernel(
         x_sb = keep.tile([P, BATCH, TILES, EMBED], BF16)
         cos_sb = keep.tile([P, TILES, HEAD_DIM], BF16)
         sin_sb = keep.tile([P, TILES, HEAD_DIM], BF16)
-        factors = keep.tile([P, 2, 2, TILES, HEAD_DIM], F32)
+        factors = keep.tile([P, 2, TILES, HEAD_DIM], BF16)
         w_words = keep.tile([P, 2, 2 * EMBED], U8, align_bytes=64)
         w_scales = keep.tile([P, 2, EMBED], U8, align_bytes=64)
         ident = keep.tile([P, P], F32)
@@ -82,24 +84,25 @@ def tile_multiscaleretention_pa_t_kernel(
         def build_factors(rows):
             even = slice(0, HEAD_DIM, 2)
             odd = slice(1, HEAD_DIM, 2)
-            for w, scale in enumerate(OUT_SCALE):
-                nc.scalar.mul(out=factors[:, w, 0, rows, even], in_=cos_sb[:, rows, even], mul=scale)
-                nc.scalar.mul(out=factors[:, w, 0, rows, odd], in_=sin_sb[:, rows, odd], mul=scale)
-                nc.scalar.mul(out=factors[:, w, 1, rows, even], in_=sin_sb[:, rows, even], mul=-scale)
-                nc.scalar.mul(out=factors[:, w, 1, rows, odd], in_=cos_sb[:, rows, odd], mul=scale)
+            nc.scalar.copy(out=factors[:, 0, rows, even], in_=cos_sb[:, rows, even])
+            nc.scalar.copy(out=factors[:, 0, rows, odd], in_=sin_sb[:, rows, odd])
+            nc.scalar.mul(out=factors[:, 1, rows, even], in_=sin_sb[:, rows, even], mul=-1.0)
+            nc.scalar.copy(out=factors[:, 1, rows, odd], in_=cos_sb[:, rows, odd])
 
         def regroup(n):
             first, b = groups[n]
-            xt = psum_t.tile([P, GROUP, 2, P], F32)
-            for j in range(GROUP):
-                words = x_sb[:, b, first + j, :].bitcast(F32)
-                for half in range(2):
-                    nc.tensor.transpose(xt[:, j, half, :], words[:, half:WORDS:2], ident[:])
             grouped = stage.tile([P, GROUP * P * 4], BF16, align_bytes=64)
-            nc.scalar.copy(
-                out=grouped[:].bitcast(F32).rearrange("p (j t h) -> p j t h", j=GROUP, h=2),
-                in_=xt[:].rearrange("p j h t -> p j t h"),
-            )
+            grouped_words = grouped[:].bitcast(F32).rearrange("p (j t h) -> p j t h", j=GROUP, h=2)
+            for j0 in range(0, GROUP, BANK_TILES):
+                xt = psum_t.tile([P, BANK_TILES, 2, P], F32)
+                for j in range(BANK_TILES):
+                    words = x_sb[:, b, first + j0 + j, :].bitcast(F32)
+                    for half in range(2):
+                        nc.tensor.transpose(xt[:, j, half, :], words[:, half:WORDS:2], ident[:])
+                nc.scalar.copy(
+                    out=grouped_words[:, j0 : j0 + BANK_TILES],
+                    in_=xt[:].rearrange("p j h t -> p j t h"),
+                )
             grouped_of[n] = grouped
             if b == 0:
                 build_factors(slice(first, first + GROUP))
@@ -130,23 +133,23 @@ def tile_multiscaleretention_pa_t_kernel(
                         start=True,
                         stop=True,
                     )
-                    shape = [P, 2, HEADS, PAIRS, 2]
-                    nc.vector.tensor_tensor(
-                        out=products[:, :, :, j, :].rearrange("p e h (i r) -> p e h i r", r=2),
-                        in0=u[:]
-                        .rearrange("p (h i e) -> p e h i", h=HEADS, e=2)
-                        .unsqueeze(4)
-                        .to_broadcast(shape),
-                        in1=factors[:, w, :, first + j, :]
-                        .rearrange("p e (i r) -> p e i r", r=2)
-                        .unsqueeze(2)
-                        .to_broadcast(shape),
-                        op=MULT,
-                    )
+                    pairs = u[:].rearrange("p (h i e) -> p h i e", h=HEADS, e=2)
+                    for e in range(2):
+                        nc.vector.scalar_tensor_tensor(
+                            out=products[:, e, :, j, :].rearrange("p h (i r) -> p h i r", r=2),
+                            in0=pairs[:, :, :, e : e + 1].to_broadcast([P, HEADS, PAIRS, 2]),
+                            scalar=OUT_SCALE[w],
+                            in1=factors[:, e, first + j, :]
+                            .rearrange("p (i r) -> p i r", r=2)
+                            .unsqueeze(1)
+                            .to_broadcast([P, HEADS, PAIRS, 2]),
+                            op0=MULT,
+                            op1=MULT,
+                        )
                 rotated = results.tile([P, HEADS, GROUP, HEAD_DIM], F32)
-                nc.gpsimd.tensor_tensor(
-                    out=rotated[:], in0=products[:, 0], in1=products[:, 1], op=ADD
-                )
+                adds_left = 2 * (len(groups) - n) - w
+                adder = nc.vector if adds_left <= VECTOR_ADDS else nc.gpsimd
+                adder.tensor_tensor(out=rotated[:], in0=products[:, 0], in1=products[:, 1], op=ADD)
                 nc.sync.dma_start(
                     out=dst[b].rearrange("h (p j) c -> p h j c", j=TILES)[:, :, rows, :],
                     in_=rotated[:],

@@ -19,8 +19,12 @@ HEAD_DIM = EMBED // HEADS
 PAIRS = HEAD_DIM // 2
 TILES = SEQ // P
 GROUP = 4
+SETS = TILES // GROUP
 BANK_TILES = 2
-VECTOR_ADDS = 1
+UNIT = 2
+PAIR = 2
+PAIR_STEPS = 3
+FEED_STEPS = 2
 WORDS = EMBED // 2
 OUT_SCALE = (1.0, HEAD_DIM**-0.5)
 
@@ -31,35 +35,49 @@ def tile_multiscaleretention_pa_t_kernel(
     tc, x, sin, cos, Wq_words, Wq_scales, Wk_words, Wk_scales, out_0, out_1
 ):
     nc = tc.nc
-    groups = [(first, b) for first in range(0, TILES, GROUP) for b in range(BATCH)]
+    outs = (out_0, out_1)
+    even = slice(0, HEAD_DIM, 2)
+    odd = slice(1, HEAD_DIM, 2)
+    turned_groups = [(first, b) for first in range(0, TILES - GROUP, GROUP) for b in range(BATCH)]
+    straight_groups = [(TILES - GROUP, b) for b in range(BATCH)]
 
     with ExitStack() as ctx:
         keep = ctx.enter_context(tc.tile_pool(name="keep", bufs=1))
-        stage = ctx.enter_context(tc.tile_pool(name="stage", bufs=3))
-        work = ctx.enter_context(tc.tile_pool(name="work", bufs=3))
+        stage = ctx.enter_context(tc.tile_pool(name="stage", bufs=4))
+        work = ctx.enter_context(tc.tile_pool(name="work", bufs=6))
+        slow = ctx.enter_context(tc.tile_pool(name="slow", bufs=2))
+        fed_sums = ctx.enter_context(tc.tile_pool(name="fed_sums", bufs=8))
         results = ctx.enter_context(tc.tile_pool(name="results", bufs=4))
         psum_t = ctx.enter_context(tc.psum_pool(name="psum_t", bufs=2))
-        psum_u = ctx.enter_context(tc.psum_pool(name="psum_u", bufs=6))
+        psum_u = ctx.enter_context(tc.psum_pool(name="psum_u", bufs=4))
+        psum_b = ctx.enter_context(tc.psum_pool(name="psum_b", bufs=2))
 
         x_sb = keep.tile([P, BATCH, TILES, EMBED], BF16)
         cos_sb = keep.tile([P, TILES, HEAD_DIM], BF16)
         sin_sb = keep.tile([P, TILES, HEAD_DIM], BF16)
-        factors = keep.tile([P, 2, TILES, HEAD_DIM], BF16)
+        crossed = keep.tile([P, TILES, HEAD_DIM], BF16)
+        tables_t = keep.tile([P, SETS, 2, GROUP * P], BF16)
+        factors = keep.tile([P, 2, GROUP, HEAD_DIM], BF16)
         w_words = keep.tile([P, 2, 2 * EMBED], U8, align_bytes=64)
         w_scales = keep.tile([P, 2, EMBED], U8, align_bytes=64)
         ident = keep.tile([P, P], F32)
+        swap = keep.tile([P, P], F32)
+        ident_bf = keep.tile([P, P], BF16)
 
         x_rows = x.rearrange("b (p j) k -> b p j k", j=TILES)
         cos_rows = cos.rearrange("(p j) c -> p j c", j=TILES)
         sin_rows = sin.rearrange("(p j) c -> p j c", j=TILES)
 
-        def load_group(n):
-            first, b = groups[n]
+        def load_group(g, pieces=1):
+            first, b = g
+            for j0 in range(first, first + GROUP, GROUP // pieces):
+                rows = slice(j0, j0 + GROUP // pieces)
+                nc.sync.dma_start(out=x_sb[:, b, rows, :], in_=x_rows[b, :, rows, :])
+
+        def load_tables(first):
             rows = slice(first, first + GROUP)
-            nc.sync.dma_start(out=x_sb[:, b, rows, :], in_=x_rows[b, :, rows, :])
-            if b == 0:
-                nc.sync.dma_start(out=cos_sb[:, rows, :], in_=cos_rows[:, rows, :])
-                nc.sync.dma_start(out=sin_sb[:, rows, :], in_=sin_rows[:, rows, :])
+            nc.sync.dma_start(out=sin_sb[:, rows, :], in_=sin_rows[:, rows, :])
+            nc.sync.dma_start(out=cos_sb[:, rows, :], in_=cos_rows[:, rows, :])
 
         def load_weight(w, words, scales):
             nc.sync.dma_start(out=w_words[:, w, :].bitcast(I32), in_=words[0].bitcast(I32))
@@ -69,98 +87,247 @@ def tile_multiscaleretention_pa_t_kernel(
                     in_=scales[0, 4 * quad : 4 * quad + 4, :].bitcast(I32),
                 )
 
+        ctx.enter_context(tc.manual_schedule())
+
         nc.vector.memset(w_scales[:].bitcast(I32), 0)
         make_identity(nc, ident[:])
+        make_identity(nc, ident_bf[:])
+        nc.scalar.copy(out=swap[:, 0:P:2], in_=ident[:, 1:P:2])
+        nc.scalar.copy(out=swap[:, 1:P:2], in_=ident[:, 0:P:2])
 
-        load_group(0)
+        load_group(turned_groups[0], pieces=2)
+        load_tables(0)
         load_weight(0, Wq_words, Wq_scales)
         load_weight(1, Wk_words, Wk_scales)
-        for n in range(1, len(groups)):
-            load_group(n)
+        load_group(straight_groups[0])
+        load_tables(straight_groups[0][0])
+        load_group(turned_groups[1])
+        for first in range(GROUP, TILES - GROUP, GROUP):
+            load_tables(first)
+        load_group(turned_groups[2])
+        load_group(straight_groups[1])
+        for g in turned_groups[3:]:
+            load_group(g)
 
         grouped_of = {}
         codes_of = {}
+        sums_of = {}
+        products_of = {}
+        rotated_of = {}
 
-        def build_factors(rows):
-            even = slice(0, HEAD_DIM, 2)
-            odd = slice(1, HEAD_DIM, 2)
-            nc.scalar.copy(out=factors[:, 0, rows, even], in_=cos_sb[:, rows, even])
-            nc.scalar.copy(out=factors[:, 0, rows, odd], in_=sin_sb[:, rows, odd])
-            nc.scalar.mul(out=factors[:, 1, rows, even], in_=sin_sb[:, rows, even], mul=-1.0)
-            nc.scalar.copy(out=factors[:, 1, rows, odd], in_=cos_sb[:, rows, odd])
-
-        def regroup(n):
-            first, b = groups[n]
-            grouped = stage.tile([P, GROUP * P * 4], BF16, align_bytes=64)
+        def regroup(g, copiers):
+            first, b = g
+            grouped = stage.tile([P, GROUP * P * 4], BF16, align_bytes=64, tag="grouped")
             grouped_words = grouped[:].bitcast(F32).rearrange("p (j t h) -> p j t h", j=GROUP, h=2)
             for j0 in range(0, GROUP, BANK_TILES):
-                xt = psum_t.tile([P, BANK_TILES, 2, P], F32)
+                xt = psum_t.tile([P, BANK_TILES, 2, P], F32, tag="xt")
                 for j in range(BANK_TILES):
                     words = x_sb[:, b, first + j0 + j, :].bitcast(F32)
                     for half in range(2):
                         nc.tensor.transpose(xt[:, j, half, :], words[:, half:WORDS:2], ident[:])
-                nc.scalar.copy(
+                copiers[j0 // BANK_TILES](
                     out=grouped_words[:, j0 : j0 + BANK_TILES],
                     in_=xt[:].rearrange("p j h t -> p j t h"),
                 )
-            grouped_of[n] = grouped
-            if b == 0:
-                build_factors(slice(first, first + GROUP))
+            grouped_of[g] = grouped
 
-        def quantise(n):
-            codes = stage.tile([P, GROUP * P], U32, align_bytes=64)
-            scales = stage.tile([P, GROUP * P], U8, align_bytes=64)
+        def quantise(g):
+            codes = stage.tile([P, GROUP * P], U32, align_bytes=64, tag="codes")
+            scales = stage.tile([P, GROUP * P], U8, align_bytes=64, tag="scales")
             nc.vector.quantize_mx(
-                out=codes[:].bitcast(FP8X4), scales=scales[:], in_=grouped_of[n][:]
+                out=codes[:].bitcast(FP8X4), scales=scales[:], in_=grouped_of[g][:]
             )
-            codes_of[n] = (codes, scales)
+            codes_of[g] = (codes, scales)
 
-        def project_and_rotate(n):
-            first, b = groups[n]
-            codes, scales = codes_of[n]
+        def cross(first, on_vector):
             rows = slice(first, first + GROUP)
-            for w, dst in enumerate((out_0, out_1)):
-                products = work.tile([P, 2, HEADS, GROUP, HEAD_DIM], F32)
+            if on_vector:
+                nc.vector.tensor_copy(out=crossed[:, rows, even], in_=sin_sb[:, rows, odd])
+                nc.vector.tensor_scalar_mul(
+                    out=crossed[:, rows, odd], in0=sin_sb[:, rows, even], scalar1=-1.0
+                )
+            else:
+                nc.scalar.copy(out=crossed[:, rows, even], in_=sin_sb[:, rows, odd])
+                nc.scalar.mul(out=crossed[:, rows, odd], in_=sin_sb[:, rows, even], mul=-1.0)
+
+        def turn_tables(first, copiers):
+            for e, table in enumerate((cos_sb, crossed)):
+                tt = psum_t.tile([P, GROUP, P], BF16, tag="xt")
                 for j in range(GROUP):
-                    tokens = slice(j * P, (j + 1) * P)
-                    u = psum_u.tile([P, EMBED], F32)
-                    nc.tensor.matmul_mx(
-                        out=u[:],
-                        lhsT=codes[:, tokens].bitcast(FP8X4),
-                        lhsT_scale=scales[:, tokens],
-                        rhs=w_words[:, w, :].bitcast(FP4X4),
-                        rhs_scale=w_scales[:, w, :],
-                        start=True,
-                        stop=True,
-                    )
-                    pairs = u[:].rearrange("p (h i e) -> p h i e", h=HEADS, e=2)
-                    for e in range(2):
-                        nc.vector.scalar_tensor_tensor(
-                            out=products[:, e, :, j, :].rearrange("p h (i r) -> p h i r", r=2),
-                            in0=pairs[:, :, :, e : e + 1].to_broadcast([P, HEADS, PAIRS, 2]),
-                            scalar=OUT_SCALE[w],
-                            in1=factors[:, e, first + j, :]
-                            .rearrange("p (i r) -> p i r", r=2)
-                            .unsqueeze(1)
-                            .to_broadcast([P, HEADS, PAIRS, 2]),
-                            op0=MULT,
-                            op1=MULT,
-                        )
-                rotated = results.tile([P, HEADS, GROUP, HEAD_DIM], F32)
-                adds_left = 2 * (len(groups) - n) - w
-                adder = nc.vector if adds_left <= VECTOR_ADDS else nc.gpsimd
-                adder.tensor_tensor(out=rotated[:], in0=products[:, 0], in1=products[:, 1], op=ADD)
-                nc.sync.dma_start(
-                    out=dst[b].rearrange("h (p j) c -> p h j c", j=TILES)[:, :, rows, :],
-                    in_=rotated[:],
+                    nc.tensor.transpose(tt[:, j, :], table[:, first + j, :], ident_bf[:])
+                copiers[e](
+                    out=tables_t[:, first // GROUP, e, :], in_=tt[:].rearrange("p j t -> p (j t)")
                 )
 
-        regroup(0)
-        regroup(1)
-        quantise(0)
-        for n in range(len(groups)):
-            if n + 2 < len(groups):
-                regroup(n + 2)
-            if n + 1 < len(groups):
-                quantise(n + 1)
-            project_and_rotate(n)
+        def project_turned(bank):
+            g, w, h = bank
+            codes, scales = codes_of[g]
+            u = psum_u.tile([P, GROUP * P], F32, tag="u")
+            nc.tensor.matmul_mx(
+                out=u[:],
+                lhsT=w_words[:, w, 2 * HEAD_DIM * h : 2 * HEAD_DIM * (h + 1)].bitcast(FP4X4),
+                lhsT_scale=w_scales[:, w, HEAD_DIM * h : HEAD_DIM * (h + 1)],
+                rhs=codes[:].bitcast(FP8X4),
+                rhs_scale=scales[:],
+                start=True,
+                stop=True,
+            )
+            sums_of[bank] = u
+
+        def multiply_turned(bank):
+            g, w, h = bank
+            products = work.tile([P, 2, GROUP * P], F32, tag="products")
+            for e in range(2):
+                nc.vector.scalar_tensor_tensor(
+                    out=products[:, e, :],
+                    in0=sums_of[bank][:],
+                    scalar=OUT_SCALE[w],
+                    in1=tables_t[:, g[0] // GROUP, e, :],
+                    op0=MULT,
+                    op1=MULT,
+                )
+            products_of[bank] = products
+
+        def add_back(unit):
+            g, w, h0 = unit[0]
+            first, b = g
+            rotated = results.tile([P, UNIT, GROUP, HEAD_DIM], F32, tag="rotated")
+            for n, bank in enumerate(unit):
+                products = products_of[bank]
+                back = psum_b.tile([P, GROUP, HEAD_DIM], F32, tag="back")
+                for j in range(GROUP):
+                    tokens = slice(j * P, (j + 1) * P)
+                    nc.tensor.matmul(
+                        out=back[:, j, :], lhsT=products[:, 0, tokens], rhs=ident[:],
+                        is_transpose=True, start=True, stop=False,
+                    )
+                    nc.tensor.matmul(
+                        out=back[:, j, :], lhsT=products[:, 1, tokens], rhs=swap[:],
+                        is_transpose=True, start=False, stop=True,
+                    )
+                nc.scalar.copy(out=rotated[:, n], in_=back[:])
+            nc.sync.dma_start(
+                out=outs[w][b].rearrange("h (p j) c -> p h j c", j=TILES)[
+                    :, h0 : h0 + UNIT, first : first + GROUP, :
+                ],
+                in_=rotated[:],
+            )
+
+        def build_factors(first):
+            rows = slice(first, first + GROUP)
+            nc.scalar.copy(out=factors[:, 0, :, even], in_=cos_sb[:, rows, even])
+            nc.scalar.copy(out=factors[:, 0, :, odd], in_=sin_sb[:, rows, odd])
+            nc.scalar.mul(out=factors[:, 1, :, even], in_=sin_sb[:, rows, even], mul=-1.0)
+            nc.scalar.copy(out=factors[:, 1, :, odd], in_=cos_sb[:, rows, odd])
+
+        def project_straight(pair):
+            g, w, j0 = pair
+            codes, scales = codes_of[g]
+            sums = fed_sums.tile([P, PAIR, EMBED], F32, tag="sums")
+            for j in range(PAIR):
+                tokens = slice((j0 + j) * P, (j0 + j + 1) * P)
+                u = psum_t.tile([P, EMBED], F32, tag="xt")
+                nc.tensor.matmul_mx(
+                    out=u[:],
+                    lhsT=codes[:, tokens].bitcast(FP8X4),
+                    lhsT_scale=scales[:, tokens],
+                    rhs=w_words[:, w, :].bitcast(FP4X4),
+                    rhs_scale=w_scales[:, w, :],
+                    start=True,
+                    stop=True,
+                )
+                nc.scalar.mul(out=sums[:, j, :], in_=u[:], mul=OUT_SCALE[w])
+            sums_of[pair] = sums
+
+        def rotate_straight(pair):
+            g, w, j0 = pair
+            first, b = g
+            shape = [P, PAIR, HEADS, PAIRS, 2]
+            products = slow.tile([P, 2, PAIR, HEADS, HEAD_DIM], F32, tag="slow_products")
+            pairs = sums_of[pair][:].rearrange("p j (h i e) -> p j h i e", h=HEADS, e=2)
+            for e in range(2):
+                nc.gpsimd.tensor_tensor(
+                    out=products[:, e].rearrange("p j h (i r) -> p j h i r", r=2),
+                    in0=pairs[:, :, :, :, e : e + 1].to_broadcast(shape),
+                    in1=factors[:, e, j0 : j0 + PAIR]
+                    .rearrange("p j (i r) -> p j i r", r=2)
+                    .unsqueeze(2)
+                    .to_broadcast(shape),
+                    op=MULT,
+                )
+            if j0 == 0:
+                whole = results.tile([P, HEADS, GROUP, HEAD_DIM], F32, tag="whole")
+                rotated_of[(g, w)] = whole
+            whole = rotated_of[(g, w)]
+            nc.gpsimd.tensor_tensor(
+                out=whole[:, :, j0 : j0 + PAIR, :].rearrange("p h j c -> p j h c"),
+                in0=products[:, 0],
+                in1=products[:, 1],
+                op=ADD,
+            )
+
+        def store_straight(g, w):
+            first, b = g
+            nc.sync.dma_start(
+                out=outs[w][b].rearrange("h (p j) c -> p h j c", j=TILES)[
+                    :, :, first : first + GROUP, :
+                ],
+                in_=rotated_of[(g, w)][:],
+            )
+
+        banks = [(g, w, h) for g in turned_groups for w in range(2) for h in range(HEADS)]
+        units = [banks[i : i + UNIT] for i in range(0, len(banks), UNIT)]
+        units_a_group = 2 * HEADS // UNIT
+        pairs_list = [
+            (g, w, j0) for g in straight_groups for w in range(2) for j0 in range(0, GROUP, PAIR)
+        ]
+
+        stores_due = {}
+        regroup(turned_groups[0], (nc.vector.tensor_copy, nc.scalar.copy))
+        cross(0, True)
+        quantise(turned_groups[0])
+        turn_tables(0, (nc.vector.tensor_copy, nc.scalar.copy))
+        for step in range(len(units) + 2):
+            t, phase = divmod(step, units_a_group)
+            pair = None
+            fed = step // FEED_STEPS - 1
+            if step % FEED_STEPS == 0 and 0 <= fed < len(pairs_list):
+                pair = pairs_list[fed]
+            for g, w in stores_due.get(step, []):
+                store_straight(g, w)
+            if step < len(units):
+                for bank in units[step]:
+                    project_turned(bank)
+            if pair is not None:
+                project_straight(pair)
+            if 1 <= step <= len(units):
+                for bank in units[step - 1]:
+                    multiply_turned(bank)
+            if step == 1:
+                quantise(straight_groups[0])
+            if step == 8:
+                quantise(straight_groups[1])
+            if phase == 2 and t + 1 < len(turned_groups):
+                quantise(turned_groups[t + 1])
+            if step >= 2:
+                add_back(units[step - 2])
+            if step == 0:
+                regroup(straight_groups[0], (nc.scalar.copy, nc.scalar.copy))
+                build_factors(straight_groups[0][0])
+            if step == 7:
+                regroup(straight_groups[1], (nc.scalar.copy, nc.scalar.copy))
+            if phase == 1 and t + 1 < len(turned_groups):
+                regroup(turned_groups[t + 1], (nc.scalar.copy, nc.scalar.copy))
+                if turned_groups[t + 1][1] == 0:
+                    turn_tables(turned_groups[t + 1][0], (nc.scalar.copy, nc.scalar.copy))
+            if pair is not None:
+                rotate_straight(pair)
+                if pair[2] + PAIR == GROUP:
+                    done = FEED_STEPS + PAIR_STEPS * (fed + 1) + 1
+                    stores_due.setdefault(done, []).append(pair[:2])
+            if phase == 3 and t + 1 < SETS - 1:
+                cross((t + 1) * GROUP, False)
+        for step in sorted(stores_due):
+            if step >= len(units) + 2:
+                for g, w in stores_due[step]:
+                    store_straight(g, w)

@@ -177,15 +177,14 @@ def tile_multiscaleretention_pa_t_kernel(
         def multiply_turned(bank):
             g, w, h = bank
             products = work.tile([P, 2, GROUP * P], F32, tag="products")
-            for e in range(2):
-                nc.vector.scalar_tensor_tensor(
-                    out=products[:, e, :],
-                    in0=sums_of[bank][:],
-                    scalar=OUT_SCALE[w],
-                    in1=tables_t[:, g[0] // GROUP, e, :],
-                    op0=MULT,
-                    op1=MULT,
-                )
+            nc.vector.scalar_tensor_tensor(
+                out=products[:],
+                in0=sums_of[bank][:].unsqueeze(1).to_broadcast([P, 2, GROUP * P]),
+                scalar=OUT_SCALE[w],
+                in1=tables_t[:, g[0] // GROUP],
+                op0=MULT,
+                op1=MULT,
+            )
             products_of[bank] = products
 
         def add_back(unit):

@@ -91,7 +91,7 @@ def tile_multiscaleretention_pa_t_kernel(
 
         nc.vector.memset(w_scales[:].bitcast(I32), 0)
         make_identity(nc, ident[:])
-        make_identity(nc, ident_bf[:])
+        nc.vector.tensor_copy(out=ident_bf[:], in_=ident[:])
         nc.scalar.copy(out=swap[:, 0:P:2], in_=ident[:, 1:P:2])
         nc.scalar.copy(out=swap[:, 1:P:2], in_=ident[:, 0:P:2])
 
@@ -205,12 +205,20 @@ def tile_multiscaleretention_pa_t_kernel(
                         is_transpose=True, start=False, stop=True,
                     )
                 nc.scalar.copy(out=rotated[:, n], in_=back[:])
-            nc.sync.dma_start(
-                out=outs[w][b].rearrange("h (p j) c -> p h j c", j=TILES)[
-                    :, h0 : h0 + UNIT, first : first + GROUP, :
-                ],
-                in_=rotated[:],
-            )
+                if unit == units[-1]:
+                    nc.sync.dma_start(
+                        out=outs[w][b].rearrange("h (p j) c -> p h j c", j=TILES)[
+                            :, h0 + n : h0 + n + 1, first : first + GROUP, :
+                        ],
+                        in_=rotated[:, n : n + 1],
+                    )
+            if unit != units[-1]:
+                nc.sync.dma_start(
+                    out=outs[w][b].rearrange("h (p j) c -> p h j c", j=TILES)[
+                        :, h0 : h0 + UNIT, first : first + GROUP, :
+                    ],
+                    in_=rotated[:],
+                )
 
         def build_factors(first):
             rows = slice(first, first + GROUP)

from contextlib import ExitStack

import concourse.mybir as mybir
from concourse.masks import make_identity

F32 = mybir.dt.float32
BF16 = mybir.dt.bfloat16
I32 = mybir.dt.int32
U32 = mybir.dt.uint32
U8 = mybir.dt.uint8
FP8X4 = mybir.dt.float8_e4m3fn_x4
FP4X4 = mybir.dt.float4_e2m1fn_x4
MULT = mybir.AluOpType.mult
ADD = mybir.AluOpType.add

P = 128
BATCH, SEQ, EMBED, HEADS = 2, 2048, 512, 4
HEAD_DIM = EMBED // HEADS
PAIRS = HEAD_DIM // 2
TILES = SEQ // P
GROUP = 4
SETS = TILES // GROUP
BANK_TILES = 2
UNIT = 2
PAIR = 2
PAIR_STEPS = 3
FEED_STEPS = 2
WORDS = EMBED // 2
OUT_SCALE = (1.0, HEAD_DIM**-0.5)

FLOPS = 2 * BATCH * SEQ * EMBED * 2 * EMBED


def tile_multiscaleretention_pa_t_kernel(
    tc, x, sin, cos, Wq_words, Wq_scales, Wk_words, Wk_scales, out_0, out_1
):
    nc = tc.nc
    outs = (out_0, out_1)
    even = slice(0, HEAD_DIM, 2)
    odd = slice(1, HEAD_DIM, 2)
    turned_groups = [(first, b) for first in range(0, TILES - GROUP, GROUP) for b in range(BATCH)]
    straight_groups = [(TILES - GROUP, b) for b in range(BATCH)]

    with ExitStack() as ctx:
        keep = ctx.enter_context(tc.tile_pool(name="keep", bufs=1))
        stage = ctx.enter_context(tc.tile_pool(name="stage", bufs=4))
        work = ctx.enter_context(tc.tile_pool(name="work", bufs=6))
        slow = ctx.enter_context(tc.tile_pool(name="slow", bufs=2))
        fed_sums = ctx.enter_context(tc.tile_pool(name="fed_sums", bufs=8))
        results = ctx.enter_context(tc.tile_pool(name="results", bufs=4))
        psum_t = ctx.enter_context(tc.psum_pool(name="psum_t", bufs=2))
        psum_u = ctx.enter_context(tc.psum_pool(name="psum_u", bufs=4))
        psum_b = ctx.enter_context(tc.psum_pool(name="psum_b", bufs=2))

        x_sb = keep.tile([P, BATCH, TILES, EMBED], BF16)
        cos_sb = keep.tile([P, TILES, HEAD_DIM], BF16)
        sin_sb = keep.tile([P, TILES, HEAD_DIM], BF16)
        crossed = keep.tile([P, TILES, HEAD_DIM], BF16)
        tables_t = keep.tile([P, SETS, 2, GROUP * P], BF16)
        factors = keep.tile([P, 2, GROUP, HEAD_DIM], BF16)
        w_words = keep.tile([P, 2, 2 * EMBED], U8, align_bytes=64)
        w_scales = keep.tile([P, 2, EMBED], U8, align_bytes=64)
        ident = keep.tile([P, P], F32)
        swap = keep.tile([P, P], F32)
        ident_bf = keep.tile([P, P], BF16)

        x_rows = x.rearrange("b (p j) k -> b p j k", j=TILES)
        cos_rows = cos.rearrange("(p j) c -> p j c", j=TILES)
        sin_rows = sin.rearrange("(p j) c -> p j c", j=TILES)

        def load_group(g, pieces=1):
            first, b = g
            for j0 in range(first, first + GROUP, GROUP // pieces):
                rows = slice(j0, j0 + GROUP // pieces)
                nc.sync.dma_start(out=x_sb[:, b, rows, :], in_=x_rows[b, :, rows, :])

        def load_tables(first):
            rows = slice(first, first + GROUP)
            nc.sync.dma_start(out=sin_sb[:, rows, :], in_=sin_rows[:, rows, :])
            nc.sync.dma_start(out=cos_sb[:, rows, :], in_=cos_rows[:, rows, :])

        def load_weight(w, words, scales):
            nc.sync.dma_start(out=w_words[:, w, :].bitcast(I32), in_=words[0].bitcast(I32))
            for quad in range(4):
                nc.sync.dma_start(
                    out=w_scales[32 * quad : 32 * quad + 4, w, :].bitcast(I32),
                    in_=scales[0, 4 * quad : 4 * quad + 4, :].bitcast(I32),
                )

        ctx.enter_context(tc.manual_schedule())

        nc.vector.memset(w_scales[:].bitcast(I32), 0)
        make_identity(nc, ident[:])
        nc.vector.tensor_copy(out=ident_bf[:], in_=ident[:])
        nc.scalar.copy(out=swap[:, 0:P:2], in_=ident[:, 1:P:2])
        nc.scalar.copy(out=swap[:, 1:P:2], in_=ident[:, 0:P:2])

        load_group(turned_groups[0], pieces=2)
        load_tables(0)
        load_weight(0, Wq_words, Wq_scales)
        load_weight(1, Wk_words, Wk_scales)
        load_group(straight_groups[0])
        load_tables(straight_groups[0][0])
        load_group(turned_groups[1])
        for first in range(GROUP, TILES - GROUP, GROUP):
            load_tables(first)
        load_group(turned_groups[2])
        load_group(straight_groups[1])
        for g in turned_groups[3:]:
            load_group(g)

        grouped_of = {}
        codes_of = {}
        sums_of = {}
        products_of = {}
        rotated_of = {}

        def regroup(g, copiers):
            first, b = g
            grouped = stage.tile([P, GROUP * P * 4], BF16, align_bytes=64, tag="grouped")
            grouped_words = grouped[:].bitcast(F32).rearrange("p (j t h) -> p j t h", j=GROUP, h=2)
            for j0 in range(0, GROUP, BANK_TILES):
                xt = psum_t.tile([P, BANK_TILES, 2, P], F32, tag="xt")
                for j in range(BANK_TILES):
                    words = x_sb[:, b, first + j0 + j, :].bitcast(F32)
                    for half in range(2):
                        nc.tensor.transpose(xt[:, j, half, :], words[:, half:WORDS:2], ident[:])
                copiers[j0 // BANK_TILES](
                    out=grouped_words[:, j0 : j0 + BANK_TILES],
                    in_=xt[:].rearrange("p j h t -> p j t h"),
                )
            grouped_of[g] = grouped

        def quantise(g):
            codes = stage.tile([P, GROUP * P], U32, align_bytes=64, tag="codes")
            scales = stage.tile([P, GROUP * P], U8, align_bytes=64, tag="scales")
            nc.vector.quantize_mx(
                out=codes[:].bitcast(FP8X4), scales=scales[:], in_=grouped_of[g][:]
            )
            codes_of[g] = (codes, scales)

        def cross(first, on_vector):
            rows = slice(first, first + GROUP)
            if on_vector:
                nc.vector.tensor_copy(out=crossed[:, rows, even], in_=sin_sb[:, rows, odd])
                nc.vector.tensor_scalar_mul(
                    out=crossed[:, rows, odd], in0=sin_sb[:, rows, even], scalar1=-1.0
                )
            else:
                nc.scalar.copy(out=crossed[:, rows, even], in_=sin_sb[:, rows, odd])
                nc.scalar.mul(out=crossed[:, rows, odd], in_=sin_sb[:, rows, even], mul=-1.0)

        def turn_tables(first, copiers):
            for e, table in enumerate((cos_sb, crossed)):
                tt = psum_t.tile([P, GROUP, P], BF16, tag="xt")
                for j in range(GROUP):
                    nc.tensor.transpose(tt[:, j, :], table[:, first + j, :], ident_bf[:])
                copiers[e](
                    out=tables_t[:, first // GROUP, e, :], in_=tt[:].rearrange("p j t -> p (j t)")
                )

        def project_turned(bank):
            g, w, h = bank
            codes, scales = codes_of[g]
            u = psum_u.tile([P, GROUP * P], F32, tag="u")
            nc.tensor.matmul_mx(
                out=u[:],
                lhsT=w_words[:, w, 2 * HEAD_DIM * h : 2 * HEAD_DIM * (h + 1)].bitcast(FP4X4),
                lhsT_scale=w_scales[:, w, HEAD_DIM * h : HEAD_DIM * (h + 1)],
                rhs=codes[:].bitcast(FP8X4),
                rhs_scale=scales[:],
                start=True,
                stop=True,
            )
            sums_of[bank] = u

        def multiply_turned(bank):
            g, w, h = bank
            products = work.tile([P, 2, GROUP * P], F32, tag="products")
            nc.vector.scalar_tensor_tensor(
                out=products[:],
                in0=sums_of[bank][:].unsqueeze(1).to_broadcast([P, 2, GROUP * P]),
                scalar=OUT_SCALE[w],
                in1=tables_t[:, g[0] // GROUP],
                op0=MULT,
                op1=MULT,
            )
            products_of[bank] = products

        def add_back(unit):
            g, w, h0 = unit[0]
            first, b = g
            rotated = results.tile([P, UNIT, GROUP, HEAD_DIM], F32, tag="rotated")
            for n, bank in enumerate(unit):
                products = products_of[bank]
                back = psum_b.tile([P, GROUP, HEAD_DIM], F32, tag="back")
                for j in range(GROUP):
                    tokens = slice(j * P, (j + 1) * P)
                    nc.tensor.matmul(
                        out=back[:, j, :], lhsT=products[:, 0, tokens], rhs=ident[:],
                        is_transpose=True, start=True, stop=False,
                    )
                    nc.tensor.matmul(
                        out=back[:, j, :], lhsT=products[:, 1, tokens], rhs=swap[:],
                        is_transpose=True, start=False, stop=True,
                    )
                nc.scalar.copy(out=rotated[:, n], in_=back[:])
                if unit == units[-1]:
                    nc.sync.dma_start(
                        out=outs[w][b].rearrange("h (p j) c -> p h j c", j=TILES)[
                            :, h0 + n : h0 + n + 1, first : first + GROUP, :
                        ],
                        in_=rotated[:, n : n + 1],
                    )
            if unit != units[-1]:
                nc.sync.dma_start(
                    out=outs[w][b].rearrange("h (p j) c -> p h j c", j=TILES)[
                        :, h0 : h0 + UNIT, first : first + GROUP, :
                    ],
                    in_=rotated[:],
                )

        def build_factors(first):
            rows = slice(first, first + GROUP)
            nc.scalar.copy(out=factors[:, 0, :, even], in_=cos_sb[:, rows, even])
            nc.scalar.copy(out=factors[:, 0, :, odd], in_=sin_sb[:, rows, odd])
            nc.scalar.mul(out=factors[:, 1, :, even], in_=sin_sb[:, rows, even], mul=-1.0)
            nc.scalar.copy(out=factors[:, 1, :, odd], in_=cos_sb[:, rows, odd])

        def project_straight(pair):
            g, w, j0 = pair
            codes, scales = codes_of[g]
            sums = fed_sums.tile([P, PAIR, EMBED], F32, tag="sums")
            for j in range(PAIR):
                tokens = slice((j0 + j) * P, (j0 + j + 1) * P)
                u = psum_t.tile([P, EMBED], F32, tag="xt")
                nc.tensor.matmul_mx(
                    out=u[:],
                    lhsT=codes[:, tokens].bitcast(FP8X4),
                    lhsT_scale=scales[:, tokens],
                    rhs=w_words[:, w, :].bitcast(FP4X4),
                    rhs_scale=w_scales[:, w, :],
                    start=True,
                    stop=True,
                )
                nc.scalar.mul(out=sums[:, j, :], in_=u[:], mul=OUT_SCALE[w])
            sums_of[pair] = sums

        def rotate_straight(pair):
            g, w, j0 = pair
            first, b = g
            shape = [P, PAIR, HEADS, PAIRS, 2]
            products = slow.tile([P, 2, PAIR, HEADS, HEAD_DIM], F32, tag="slow_products")
            pairs = sums_of[pair][:].rearrange("p j (h i e) -> p j h i e", h=HEADS, e=2)
            for e in range(2):
                nc.gpsimd.tensor_tensor(
                    out=products[:, e].rearrange("p j h (i r) -> p j h i r", r=2),
                    in0=pairs[:, :, :, :, e : e + 1].to_broadcast(shape),
                    in1=factors[:, e, j0 : j0 + PAIR]
                    .rearrange("p j (i r) -> p j i r", r=2)
                    .unsqueeze(2)
                    .to_broadcast(shape),
                    op=MULT,
                )
            if j0 == 0:
                whole = results.tile([P, HEADS, GROUP, HEAD_DIM], F32, tag="whole")
                rotated_of[(g, w)] = whole
            whole = rotated_of[(g, w)]
            nc.gpsimd.tensor_tensor(
                out=whole[:, :, j0 : j0 + PAIR, :].rearrange("p h j c -> p j h c"),
                in0=products[:, 0],
                in1=products[:, 1],
                op=ADD,
            )

        def store_straight(g, w):
            first, b = g
            nc.sync.dma_start(
                out=outs[w][b].rearrange("h (p j) c -> p h j c", j=TILES)[
                    :, :, first : first + GROUP, :
                ],
                in_=rotated_of[(g, w)][:],
            )

        banks = [(g, w, h) for g in turned_groups for w in range(2) for h in range(HEADS)]
        units = [banks[i : i + UNIT] for i in range(0, len(banks), UNIT)]
        units_a_group = 2 * HEADS // UNIT
        pairs_list = [
            (g, w, j0) for g in straight_groups for w in range(2) for j0 in range(0, GROUP, PAIR)
        ]

        stores_due = {}
        regroup(turned_groups[0], (nc.vector.tensor_copy, nc.scalar.copy))
        cross(0, True)
        quantise(turned_groups[0])
        turn_tables(0, (nc.vector.tensor_copy, nc.scalar.copy))
        for step in range(len(units) + 2):
            t, phase = divmod(step, units_a_group)
            pair = None
            fed = step // FEED_STEPS - 1
            if step % FEED_STEPS == 0 and 0 <= fed < len(pairs_list):
                pair = pairs_list[fed]
            for g, w in stores_due.get(step, []):
                store_straight(g, w)
            if step < len(units):
                for bank in units[step]:
                    project_turned(bank)
            if pair is not None:
                project_straight(pair)
            if 1 <= step <= len(units):
                for bank in units[step - 1]:
                    multiply_turned(bank)
            if step == 1:
                quantise(straight_groups[0])
            if step == 8:
                quantise(straight_groups[1])
            if phase == 2 and t + 1 < len(turned_groups):
                quantise(turned_groups[t + 1])
            if step >= 2:
                add_back(units[step - 2])
            if step == 0:
                regroup(straight_groups[0], (nc.scalar.copy, nc.scalar.copy))
                build_factors(straight_groups[0][0])
            if step == 7:
                regroup(straight_groups[1], (nc.scalar.copy, nc.scalar.copy))
            if phase == 1 and t + 1 < len(turned_groups):
                regroup(turned_groups[t + 1], (nc.scalar.copy, nc.scalar.copy))
                if turned_groups[t + 1][1] == 0:
                    turn_tables(turned_groups[t + 1][0], (nc.scalar.copy, nc.scalar.copy))
            if pair is not None:
                rotate_straight(pair)
                if pair[2] + PAIR == GROUP:
                    done = FEED_STEPS + PAIR_STEPS * (fed + 1) + 1
                    stores_due.setdefault(done, []).append(pair[:2])
            if phase == 3 and t + 1 < SETS - 1:
                cross((t + 1) * GROUP, False)
        for step in sorted(stores_due):
            if step >= len(units) + 2:
                for g, w in stores_due[step]:
                    store_straight(g, w)
